import numpy as np
import ml_dtypes


def mxq(x, axis, fmt="e4m3"):
    dtype, down = {"e4m3": (ml_dtypes.float8_e4m3fn, 7), "e5m2": (ml_dtypes.float8_e5m2, 14)}[fmt]
    v = np.moveaxis(np.asarray(x, np.float32).astype(ml_dtypes.bfloat16).astype(np.float64), axis, -1)
    blocks = v.reshape(v.shape[:-1] + (-1, 32))
    amax = np.abs(blocks).max(-1, keepdims=True)
    byte = np.maximum(np.where(amax > 0, np.frexp(amax)[1] - 1 + 127, 0) - down, 1)
    scale = np.exp2(byte - 127.0)
    codes = (blocks / scale).astype(np.float32).astype(dtype).astype(np.float64)
    return np.moveaxis((codes * scale).reshape(v.shape), -1, axis)


WIDE = False


def mx_kscale(k):
    if not WIDE:
        return np.ones(k)
    levels = np.array([10, -10, 5, -5, 0])
    a = np.random.permutation(np.resize(levels, k // 512 * 4)).reshape(k // 512, 4)
    idx = np.arange(k)
    return np.exp2(a[idx // 512, idx % 128 // 32])


BF16 = ml_dtypes.bfloat16


def bf(x):
    return np.asarray(x, np.float32).astype(BF16)


def f64(x):
    return np.asarray(x).astype(np.float64)


E2M1 = np.array([0.0, 0.5, 1.0, 1.5, 2.0, 3.0, 4.0, 6.0, -0.0, -0.5, -1.0, -1.5, -2.0, -3.0, -4.0, -6.0])


def pack_weight(w, fmt):
    k, n = w.shape
    w = f64(bf(w)).reshape(k // 32, 32, n)
    amax = np.abs(w).max(1)
    if fmt == "e4m3":
        byte = np.frexp(amax)[1] - 1 + 127 - 7
    else:
        mant, ex = np.frexp(amax / 6.0)
        byte = np.where(mant > 0.5, ex, ex - 1) + 127
    byte = np.clip(np.where(amax > 0, byte, 1), 1, 254)
    scaled = (w * np.exp2(127.0 - byte)[:, None, :]).reshape(k, n).astype(np.float32)
    by_word = np.ascontiguousarray(scaled.reshape(k // 512, 128, 4, n).transpose(0, 1, 3, 2))
    if fmt == "e4m3":
        words = by_word.astype(ml_dtypes.float8_e4m3fn).view(np.uint8)
    else:
        c = by_word.astype(ml_dtypes.float4_e2m1fn).view(np.uint8) & 0xF
        words = c[..., 0::2] | (c[..., 1::2] << 4)
    return np.ascontiguousarray(words), np.ascontiguousarray(byte.astype(np.uint8).reshape(k // 512, 16, n))


def unpack_weight(words, scales, fmt):
    g, p, n, _ = words.shape
    if fmt == "e4m3":
        vals = np.ascontiguousarray(words).view(ml_dtypes.float8_e4m3fn).astype(np.float64)
    else:
        nib = np.empty((g, p, n, 4), np.uint8)
        nib[..., 0::2] = words & 0xF
        nib[..., 1::2] = words >> 4
        vals = E2M1[nib]
    vals = vals * np.repeat(np.exp2(scales.astype(np.float64) - 127.0), 8, axis=1)[..., None]
    return vals.transpose(0, 1, 3, 2).reshape(g * 512, n)

def pack4(w):
    words, scales = pack_weight(w, "e2m1")
    return words.reshape(words.shape[0], 128, -1), scales


def unpack4(words, scales):
    return unpack_weight(words.reshape(words.shape[0], 128, -1, 2), scales, "e2m1")


B, I, H = 128, 512, 1024
EPS = 1e-5


def ln(v):
    mu = v.mean(-1, keepdims=True)
    var = np.square(v - mu).mean(-1, keepdims=True)
    return (v - mu) / np.sqrt(var + EPS)


def sigmoid(v):
    return 1.0 / (1.0 + np.exp(-v))


def setup_inputs():
    s = mx_kscale(I)
    x = bf(np.random.standard_normal((B, I)) * s)
    h = bf(np.random.standard_normal((B, H)))
    r = bf(sigmoid(np.sqrt(2.0) * np.random.standard_normal((B, H))))
    z = bf(sigmoid(np.sqrt(2.0) * np.random.standard_normal((B, H))))
    W_in = np.random.standard_normal((H, I)) / np.sqrt(I) / s
    b_in = bf(np.random.standard_normal(H) * 0.5)
    W_hn = np.random.standard_normal((H, H)) / np.sqrt(H)
    b_hn = bf(np.random.standard_normal(H) * 0.5)
    W_in_words, W_in_scales = pack4(np.ascontiguousarray(W_in.T))
    W_hn_words, W_hn_scales = pack4(np.ascontiguousarray(W_hn.T))
    return {"x": x,
            "h": h,
            "r": r,
            "z": z,
            "W_in_words": W_in_words,
            "W_in_scales": W_in_scales,
            "b_in": b_in,
            "W_hn_words": W_hn_words,
            "W_hn_scales": W_hn_scales,
            "b_hn": b_hn}


def reference(x, h, r, z, W_in_words, W_in_scales, b_in, W_hn_words, W_hn_scales, b_hn):
    h = f64(h)
    r, z = f64(r), f64(z)
    i_n = ln((mxq(f64(x), 1, "e4m3") @ unpack4(W_in_words, W_in_scales)) + f64(b_in))
    h_n = ln((mxq(h, 1, "e4m3") @ unpack4(W_hn_words, W_hn_scales)) + f64(b_hn))
    n = np.tanh(i_n + r * h_n)
    return (1.0 - z) * n + z * h

@@ -1,0 +1,204 @@
+from contextlib import ExitStack
+
+import concourse.mybir as mybir
+from concourse.masks import make_identity
+
+F32 = mybir.dt.float32
+BF16 = mybir.dt.bfloat16
+I32 = mybir.dt.int32
+U32 = mybir.dt.uint32
+U8 = mybir.dt.uint8
+FP8X4 = mybir.dt.float8_e4m3fn_x4
+FP4X4 = mybir.dt.float4_e2m1fn_x4
+ALU = mybir.AluOpType
+ACT = mybir.ActivationFunctionType
+
+P = 128
+I_SIZE = 512
+H_SIZE = 1024
+EPS = 1e-5
+PACK = 4
+K_PASS = P * PACK
+PASSES = (I_SIZE + H_SIZE) // K_PASS
+WORDS = K_PASS // 2
+N_TILE = 512
+HALVES = H_SIZE // N_TILE
+QUADRANTS = 4
+
+FLOPS = 2 * P * (I_SIZE + H_SIZE) * H_SIZE
+
+
+def tile_layernormgrucell_pb_s_kernel(
+    tc, x, h, r, z, W_in_words, W_in_scales, b_in, W_hn_words, W_hn_scales, b_hn, out
+):
+    nc = tc.nc
+    with ExitStack() as ctx:
+        keep = ctx.enter_context(tc.tile_pool(name="keep", bufs=1))
+        psum = ctx.enter_context(tc.psum_pool(name="psum", bufs=8))
+
+        x_sb = keep.tile([P, I_SIZE], BF16)
+        h_sb = keep.tile([P, H_SIZE], BF16)
+        nc.scalar.dma_start(out=x_sb[:], in_=x)
+        nc.scalar.dma_start(out=h_sb[:], in_=h)
+
+        warm = keep.tile([P, 1], F32)
+        nc.vector.memset(warm[:], 0.0)
+        nc.scalar.activation(out=warm[:], in_=warm[:], func=ACT.Tanh)
+
+        w_words = keep.tile([P, PASSES, 2 * H_SIZE], U8, align_bytes=64)
+        w_scales = keep.tile([P, PASSES, H_SIZE], U8, align_bytes=64)
+        nc.vector.memset(w_scales[:].bitcast(I32), 0)
+        nc.sync.dma_start(out=w_words[:, 0, :].bitcast(I32), in_=W_in_words[0].bitcast(I32))
+        for q in range(QUADRANTS):
+            nc.sync.dma_start(
+                out=w_scales[32 * q : 32 * q + 4, 0, :].bitcast(I32),
+                in_=W_in_scales[0, 4 * q : 4 * q + 4, :].bitcast(I32),
+            )
+        nc.sync.dma_start(
+            out=w_words[:, 1:PASSES, :].bitcast(I32),
+            in_=W_hn_words.bitcast(I32).rearrange("g p n -> p g n"),
+        )
+        for q in range(QUADRANTS):
+            nc.sync.dma_start(
+                out=w_scales[32 * q : 32 * q + 4, 1:PASSES, :].bitcast(I32),
+                in_=W_hn_scales[:, 4 * q : 4 * q + 4, :].bitcast(I32).rearrange("g s n -> s g n"),
+            )
+
+        ident = keep.tile([P, P], F32)
+        make_identity(nc, ident[:])
+        minus_half = keep.tile([P, 1], F32)
+        nc.gpsimd.memset(minus_half[:], -0.5)
+
+        bias = keep.tile([P, 2, H_SIZE], BF16)
+        nc.gpsimd.dma_start(out=bias[:, 0, :], in_=b_in.partition_broadcast(P))
+        nc.gpsimd.dma_start(out=bias[:, 1, :], in_=b_hn.partition_broadcast(P))
+        z_sb = keep.tile([P, H_SIZE], BF16)
+        r_sb = keep.tile([P, H_SIZE], BF16)
+        nc.gpsimd.dma_start(out=z_sb[:], in_=z)
+        nc.gpsimd.dma_start(out=r_sb[:], in_=r)
+
+        grouped = keep.tile([P, PASSES, P * PACK], BF16, align_bytes=64)
+        a_codes = keep.tile([P, PASSES, P], U32, align_bytes=64)
+        a_scales = keep.tile([P, PASSES, P], U8, align_bytes=64)
+        pass_words = [
+            x_sb[:].bitcast(F32),
+            h_sb[:].bitcast(F32)[:, 0:WORDS],
+            h_sb[:].bitcast(F32)[:, WORDS : 2 * WORDS],
+        ]
+        for c in range(PASSES):
+            flipped = psum.tile([P, 2, P], F32, tag="bank")
+            for u in range(2):
+                nc.tensor.transpose(flipped[:, u, :], pass_words[c][:, u:WORDS:2], ident[:])
+            side_by_side = grouped[:, c, :].bitcast(F32).rearrange("p (b u) -> p b u", u=2)
+            if c % 2 == 0:
+                nc.vector.tensor_copy(out=side_by_side, in_=flipped[:].rearrange("p u b -> p b u"))
+            else:
+                nc.scalar.copy(out=side_by_side, in_=flipped[:].rearrange("p u b -> p b u"))
+            if c == 0:
+                nc.vector.quantize_mx(
+                    out=a_codes[:, 0, :].bitcast(FP8X4), scales=a_scales[:, 0, :], in_=grouped[:, 0, :]
+                )
+        nc.vector.quantize_mx(
+            out=a_codes[:, 1:PASSES, :].rearrange("p c b -> p (c b)").bitcast(FP8X4),
+            scales=a_scales[:, 1:PASSES, :].rearrange("p c b -> p (c b)"),
+            in_=grouped[:, 1:PASSES, :].rearrange("p c k -> p (c k)"),
+        )
+
+        one_minus_z = keep.tile([P, H_SIZE], F32)
+        nc.scalar.activation(out=one_minus_z[:], in_=z_sb[:], func=ACT.Copy, bias=1.0, scale=-1.0)
+        z_times_h = keep.tile([P, H_SIZE], F32)
+        nc.gpsimd.tensor_tensor(out=z_times_h[:], in0=z_sb[:], in1=h_sb[:], op=ALU.mult)
+
+        passes_of_side = [[0], [1, 2]]
+        pre = keep.tile([P, 2, H_SIZE], F32)
+        half_sum = keep.tile([P, 2, HALVES], F32)
+        neg_mean = keep.tile([P, 2], F32)
+        squares = keep.tile([P, H_SIZE], F32)
+        sq_sum = keep.tile([P, 2], F32)
+        var_eps = keep.tile([P, 2], F32)
+        rstd = keep.tile([P, 2], F32)
+        gated = keep.tile([P, H_SIZE], F32)
+        for side in range(2):
+            for j in range(HALVES):
+                acc = psum.tile([P, N_TILE], F32, tag="bank")
+                for c in passes_of_side[side]:
+                    nc.tensor.matmul_mx(
+                        out=acc[:],
+                        lhsT=a_codes[:, c, :].bitcast(FP8X4),
+                        lhsT_scale=a_scales[:, c, :],
+                        rhs=w_words[:, c, 2 * N_TILE * j : 2 * N_TILE * (j + 1)].bitcast(FP4X4),
+                        rhs_scale=w_scales[:, c, N_TILE * j : N_TILE * (j + 1)],
+                        start=(c == passes_of_side[side][0]),
+                        stop=(c == passes_of_side[side][-1]),
+                    )
+                nc.vector.scalar_tensor_tensor(
+                    out=pre[:, side, N_TILE * j : N_TILE * (j + 1)],
+                    in0=acc[:],
+                    scalar=1.0,
+                    in1=bias[:, side, N_TILE * j : N_TILE * (j + 1)],
+                    op0=ALU.mult,
+                    op1=ALU.add,
+                    accum_out=half_sum[:, side, j : j + 1],
+                )
+            nc.vector.tensor_scalar(
+                out=neg_mean[:, side : side + 1],
+                in0=half_sum[:, side, 0:1],
+                scalar1=half_sum[:, side, 1:2],
+                scalar2=-1.0 / H_SIZE,
+                op0=ALU.add,
+                op1=ALU.mult,
+            )
+            nc.scalar.activation(
+                out=squares[:],
+                in_=pre[:, side, :],
+                func=ACT.Square,
+                bias=neg_mean[:, side : side + 1],
+                scale=1.0,
+                accum_out=sq_sum[:, side : side + 1],
+            )
+            if side == 1:
+                for j in range(HALVES):
+                    nc.vector.scalar_tensor_tensor(
+                        out=gated[:, N_TILE * j : N_TILE * (j + 1)],
+                        in0=pre[:, 1, N_TILE * j : N_TILE * (j + 1)],
+                        scalar=neg_mean[:, 1:2],
+                        in1=r_sb[:, N_TILE * j : N_TILE * (j + 1)],
+                        op0=ALU.add,
+                        op1=ALU.mult,
+                    )
+            nc.gpsimd.tensor_scalar(
+                out=var_eps[:, side : side + 1],
+                in0=sq_sum[:, side : side + 1],
+                scalar1=1.0 / H_SIZE,
+                scalar2=EPS,
+                op0=ALU.mult,
+                op1=ALU.add,
+            )
+            nc.gpsimd.tensor_tensor(
+                out=rstd[:, side : side + 1], in0=var_eps[:, side : side + 1], in1=minus_half[:], op=ALU.pow
+            )
+
+        i_n = keep.tile([P, H_SIZE], F32)
+        nc.vector.tensor_scalar(
+            out=i_n[:],
+            in0=pre[:, 0, :],
+            scalar1=neg_mean[:, 0:1],
+            scalar2=rstd[:, 0:1],
+            op0=ALU.add,
+            op1=ALU.mult,
+        )
+        arg = keep.tile([P, H_SIZE], F32)
+        cand = keep.tile([P, H_SIZE], F32)
+        res = keep.tile([P, H_SIZE], F32)
+        for j in range(HALVES):
+            cols = slice(N_TILE * j, N_TILE * (j + 1))
+            nc.vector.scalar_tensor_tensor(
+                out=arg[:, cols], in0=gated[:, cols], scalar=rstd[:, 1:2], in1=i_n[:, cols],
+                op0=ALU.mult, op1=ALU.add,
+            )
+            nc.scalar.activation(out=cand[:, cols], in_=arg[:, cols], func=ACT.Tanh)
+        for j in range(HALVES):
+            cols = slice(N_TILE * j, N_TILE * (j + 1))
+            nc.vector.tensor_tensor(out=res[:, cols], in0=cand[:, cols], in1=one_minus_z[:, cols], op=ALU.mult)
+            nc.vector.tensor_tensor(out=res[:, cols], in0=res[:, cols], in1=z_times_h[:, cols], op=ALU.add)
+            nc.sync.dma_start(out=out[:, cols], in_=res[:, cols])

@@ -23,6 +23,7 @@ PASSES = (I_SIZE + H_SIZE) // K_PASS
 WORDS = K_PASS // 2
 N_TILE = 512
 HALVES = H_SIZE // N_TILE
+BIAS_WORDS = H_SIZE // 2 // P
 QUADRANTS = 4
 
 FLOPS = 2 * P * (I_SIZE + H_SIZE) * H_SIZE
@@ -69,9 +70,10 @@ def tile_layernormgrucell_pb_s_kernel(
         minus_half = keep.tile([P, 1], F32)
         nc.gpsimd.memset(minus_half[:], -0.5)
 
-        bias = keep.tile([P, 2, H_SIZE], BF16)
-        nc.gpsimd.dma_start(out=bias[:, 0, :], in_=b_in.partition_broadcast(P))
-        nc.gpsimd.dma_start(out=bias[:, 1, :], in_=b_hn.partition_broadcast(P))
+        b_in_words = keep.tile([P, BIAS_WORDS * 2], BF16)
+        b_hn_words = keep.tile([P, BIAS_WORDS * 2], BF16)
+        nc.gpsimd.dma_start(out=b_in_words[:], in_=b_in.rearrange("(w e) -> w e", w=P))
+        nc.gpsimd.dma_start(out=b_hn_words[:], in_=b_hn.rearrange("(w e) -> w e", w=P))
         z_sb = keep.tile([P, H_SIZE], BF16)
         r_sb = keep.tile([P, H_SIZE], BF16)
         nc.gpsimd.dma_start(out=z_sb[:], in_=z)
@@ -103,6 +105,18 @@ def tile_layernormgrucell_pb_s_kernel(
             scales=a_scales[:, 1:PASSES, :].rearrange("p c b -> p (c b)"),
             in_=grouped[:, 1:PASSES, :].rearrange("p c k -> p (c k)"),
         )
+
+        bias = keep.tile([P, 2, H_SIZE], BF16)
+        for side, bias_words in enumerate([b_in_words, b_hn_words]):
+            spread = psum.tile([P, BIAS_WORDS, P], F32, tag="bank")
+            for m in range(BIAS_WORDS):
+                nc.tensor.transpose(
+                    spread[:, m, :], bias_words[:].bitcast(F32)[:, m : m + 1].to_broadcast([P, P]), ident[:]
+                )
+            nc.scalar.copy(
+                out=bias[:, side, :].bitcast(F32).rearrange("p (w m) -> p w m", m=BIAS_WORDS),
+                in_=spread[:].rearrange("p m w -> p w m"),
+            )
 
         one_minus_z = keep.tile([P, H_SIZE], F32)
         nc.scalar.activation(out=one_minus_z[:], in_=z_sb[:], func=ACT.Copy, bias=1.0, scale=-1.0)

@@ -36,6 +36,7 @@ def tile_layernormgrucell_pb_s_kernel(
     with ExitStack() as ctx:
         keep = ctx.enter_context(tc.tile_pool(name="keep", bufs=1))
         psum = ctx.enter_context(tc.psum_pool(name="psum", bufs=8))
+        ctx.enter_context(tc.manual_schedule())
 
         x_sb = keep.tile([P, I_SIZE], BF16)
         h_sb = keep.tile([P, H_SIZE], BF16)
@@ -48,7 +49,8 @@ def tile_layernormgrucell_pb_s_kernel(
 
         w_words = keep.tile([P, PASSES, 2 * H_SIZE], U8, align_bytes=64)
         w_scales = keep.tile([P, PASSES, H_SIZE], U8, align_bytes=64)
-        nc.vector.memset(w_scales[:].bitcast(I32), 0)
+        nc.vector.memset(w_scales[:, 0, :].bitcast(I32), 0)
+        nc.vector.memset(w_scales[:, 1:PASSES, :].bitcast(I32), 0)
         nc.sync.dma_start(out=w_words[:, 0, :].bitcast(I32), in_=W_in_words[0].bitcast(I32))
         for q in range(QUADRANTS):
             nc.sync.dma_start(
@@ -65,19 +67,18 @@ def tile_layernormgrucell_pb_s_kernel(
                 in_=W_hn_scales[:, 4 * q : 4 * q + 4, :].bitcast(I32).rearrange("g s n -> s g n"),
             )
 
-        ident = keep.tile([P, P], F32)
-        make_identity(nc, ident[:])
-        minus_half = keep.tile([P, 1], F32)
-        nc.gpsimd.memset(minus_half[:], -0.5)
-
         b_in_words = keep.tile([P, BIAS_WORDS * 2], BF16)
         b_hn_words = keep.tile([P, BIAS_WORDS * 2], BF16)
         nc.gpsimd.dma_start(out=b_in_words[:], in_=b_in.rearrange("(w e) -> w e", w=P))
+        ident = keep.tile([P, P], F32)
+        make_identity(nc, ident[:])
         nc.gpsimd.dma_start(out=b_hn_words[:], in_=b_hn.rearrange("(w e) -> w e", w=P))
         z_sb = keep.tile([P, H_SIZE], BF16)
         r_sb = keep.tile([P, H_SIZE], BF16)
         nc.gpsimd.dma_start(out=z_sb[:], in_=z)
         nc.gpsimd.dma_start(out=r_sb[:], in_=r)
+        minus_half = keep.tile([P, 1], F32)
+        nc.gpsimd.memset(minus_half[:], -0.5)
 
         grouped = keep.tile([P, PASSES, P * PACK], BF16, align_bytes=64)
         a_codes = keep.tile([P, PASSES, P], U32, align_bytes=64)
@@ -87,27 +88,29 @@ def tile_layernormgrucell_pb_s_kernel(
             h_sb[:].bitcast(F32)[:, 0:WORDS],
             h_sb[:].bitcast(F32)[:, WORDS : 2 * WORDS],
         ]
+
+        def quantise(c):
+            nc.vector.quantize_mx(
+                out=a_codes[:, c, :].bitcast(FP8X4), scales=a_scales[:, c, :], in_=grouped[:, c, :]
+            )
+
         for c in range(PASSES):
             flipped = psum.tile([P, 2, P], F32, tag="bank")
             for u in range(2):
                 nc.tensor.transpose(flipped[:, u, :], pass_words[c][:, u:WORDS:2], ident[:])
             side_by_side = grouped[:, c, :].bitcast(F32).rearrange("p (b u) -> p b u", u=2)
-            if c % 2 == 0:
+            if c == 2:
                 nc.vector.tensor_copy(out=side_by_side, in_=flipped[:].rearrange("p u b -> p b u"))
             else:
                 nc.scalar.copy(out=side_by_side, in_=flipped[:].rearrange("p u b -> p b u"))
             if c == 0:
-                nc.vector.quantize_mx(
-                    out=a_codes[:, 0, :].bitcast(FP8X4), scales=a_scales[:, 0, :], in_=grouped[:, 0, :]
-                )
-        nc.vector.quantize_mx(
-            out=a_codes[:, 1:PASSES, :].rearrange("p c b -> p (c b)").bitcast(FP8X4),
-            scales=a_scales[:, 1:PASSES, :].rearrange("p c b -> p (c b)"),
-            in_=grouped[:, 1:PASSES, :].rearrange("p c k -> p (c k)"),
-        )
+                quantise(0)
+        quantise(1)
+        quantise(2)
 
         bias = keep.tile([P, 2, H_SIZE], BF16)
-        for side, bias_words in enumerate([b_in_words, b_hn_words]):
+
+        def spread_bias(side, bias_words):
             spread = psum.tile([P, BIAS_WORDS, P], F32, tag="bank")
             for m in range(BIAS_WORDS):
                 nc.tensor.transpose(
@@ -118,101 +121,146 @@ def tile_layernormgrucell_pb_s_kernel(
                 in_=spread[:].rearrange("p m w -> p w m"),
             )
 
-        one_minus_z = keep.tile([P, H_SIZE], F32)
-        nc.scalar.activation(out=one_minus_z[:], in_=z_sb[:], func=ACT.Copy, bias=1.0, scale=-1.0)
-        z_times_h = keep.tile([P, H_SIZE], F32)
-        nc.gpsimd.tensor_tensor(out=z_times_h[:], in0=z_sb[:], in1=h_sb[:], op=ALU.mult)
-
         passes_of_side = [[0], [1, 2]]
         pre = keep.tile([P, 2, H_SIZE], F32)
-        half_sum = keep.tile([P, 2, HALVES], F32)
-        neg_mean = keep.tile([P, 2], F32)
-        squares = keep.tile([P, H_SIZE], F32)
-        sq_sum = keep.tile([P, 2], F32)
-        var_eps = keep.tile([P, 2], F32)
-        rstd = keep.tile([P, 2], F32)
-        gated = keep.tile([P, H_SIZE], F32)
-        for side in range(2):
-            for j in range(HALVES):
-                acc = psum.tile([P, N_TILE], F32, tag="bank")
-                for c in passes_of_side[side]:
-                    nc.tensor.matmul_mx(
-                        out=acc[:],
-                        lhsT=a_codes[:, c, :].bitcast(FP8X4),
-                        lhsT_scale=a_scales[:, c, :],
-                        rhs=w_words[:, c, 2 * N_TILE * j : 2 * N_TILE * (j + 1)].bitcast(FP4X4),
-                        rhs_scale=w_scales[:, c, N_TILE * j : N_TILE * (j + 1)],
-                        start=(c == passes_of_side[side][0]),
-                        stop=(c == passes_of_side[side][-1]),
-                    )
-                nc.vector.scalar_tensor_tensor(
-                    out=pre[:, side, N_TILE * j : N_TILE * (j + 1)],
-                    in0=acc[:],
-                    scalar=1.0,
-                    in1=bias[:, side, N_TILE * j : N_TILE * (j + 1)],
-                    op0=ALU.mult,
-                    op1=ALU.add,
-                    accum_out=half_sum[:, side, j : j + 1],
+        sums = keep.tile([P, 2, 4], F32)
+        squares = keep.tile([P, 2, H_SIZE], F32)
+        sq_sums = keep.tile([P, 2, 4], F32)
+
+        def product(side, cols):
+            width = cols.stop - cols.start
+            acc = psum.tile([P, width], F32, tag="bank")
+            for c in passes_of_side[side]:
+                nc.tensor.matmul_mx(
+                    out=acc[:],
+                    lhsT=a_codes[:, c, :].bitcast(FP8X4),
+                    lhsT_scale=a_scales[:, c, :],
+                    rhs=w_words[:, c, 2 * cols.start : 2 * cols.stop].bitcast(FP4X4),
+                    rhs_scale=w_scales[:, c, cols],
+                    start=(c == passes_of_side[side][0]),
+                    stop=(c == passes_of_side[side][-1]),
                 )
+            return acc
+
+        def add_bias(side, i, acc):
+            cols = pieces[side][i]
+            nc.vector.scalar_tensor_tensor(
+                out=pre[:, side, cols],
+                in0=acc[:],
+                scalar=1.0,
+                in1=bias[:, side, cols],
+                op0=ALU.mult,
+                op1=ALU.add,
+                accum_out=sums[:, side, i : i + 1],
+            )
+
+        def rstd_of(side, square_sum, mean_square_scale, rest):
+            tiny = keep.tile([P, 2], F32, tag=f"tiny{side}")
+            nc.gpsimd.tensor_scalar(
+                out=tiny[:, 0:1], in0=square_sum, scalar1=mean_square_scale, scalar2=rest,
+                op0=ALU.mult, op1=ALU.add,
+            )
+            nc.gpsimd.tensor_tensor(out=tiny[:, 1:2], in0=tiny[:, 0:1], in1=minus_half[:], op=ALU.pow)
+            return tiny[:, 1:2]
+
+        def negative_mean(side):
             nc.vector.tensor_scalar(
-                out=neg_mean[:, side : side + 1],
-                in0=half_sum[:, side, 0:1],
-                scalar1=half_sum[:, side, 1:2],
-                scalar2=-1.0 / H_SIZE,
+                out=neg_mean[:, side : side + 1], in0=sums[:, side, 0:1], scalar1=sums[:, side, 1:2],
+                scalar2=-1.0 / H_SIZE, op0=ALU.add, op1=ALU.mult,
+            )
+            return neg_mean[:, side : side + 1]
+
+        half = [slice(0, N_TILE), slice(N_TILE, H_SIZE)]
+        thirds = [slice(0, 512), slice(512, 768), slice(768, 1024)]
+        pieces = [half, half]
+        neg_mean = keep.tile([P, 2], F32)
+
+        spread_bias(0, b_in_words)
+        acc_in = [product(0, cols) for cols in half]
+        spread_bias(1, b_hn_words)
+        acc_hn = [product(1, cols) for cols in half]
+
+        z_times_h = keep.tile([P, H_SIZE], F32)
+
+        def state_term(cols):
+            nc.vector.tensor_tensor(out=z_times_h[:, cols], in0=z_sb[:, cols], in1=h_sb[:, cols], op=ALU.mult)
+
+        add_bias(0, 0, acc_in[0])
+        add_bias(0, 1, acc_in[1])
+        negative_mean(0)
+        nc.scalar.activation(
+            out=squares[:, 0, :], in_=pre[:, 0, :], func=ACT.Square, bias=neg_mean[:, 0:1], scale=1.0,
+            accum_out=sq_sums[:, 0, 0:1],
+        )
+        rstd_in = rstd_of(0, sq_sums[:, 0, 0:1], 1.0 / H_SIZE, EPS)
+        shift = keep.tile([P, 1], F32)
+        nc.gpsimd.tensor_scalar(out=shift[:], in0=neg_mean[:, 0:1], scalar1=rstd_in, scalar2=None, op0=ALU.mult)
+
+        to_var = 1.0 / (N_TILE * N_TILE * H_SIZE)
+        for j in range(HALVES):
+            add_bias(1, j, acc_hn[j])
+            nc.scalar.activation(
+                out=squares[:, 1, half[j]], in_=pre[:, 1, half[j]], func=ACT.Square,
+                bias=sums[:, 1, j : j + 1], scale=-float(N_TILE), accum_out=sq_sums[:, 1, j : j + 1],
+            )
+        state_term(half[0])
+        between = keep.tile([P, 2], F32)
+        nc.vector.tensor_scalar(
+            out=between[:, 0:1], in0=sums[:, 1, 0:1], scalar1=sums[:, 1, 1:2], scalar2=1.0 / H_SIZE,
+            op0=ALU.subtract, op1=ALU.mult,
+        )
+        negative_mean(1)
+        nc.vector.tensor_scalar(
+            out=between[:, 1:2], in0=between[:, 0:1], scalar1=between[:, 0:1], scalar2=EPS,
+            op0=ALU.mult, op1=ALU.add,
+        )
+        first_var = keep.tile([P, 1], F32)
+        nc.gpsimd.tensor_scalar(
+            out=first_var[:], in0=sq_sums[:, 1, 0:1], scalar1=to_var, scalar2=between[:, 1:2],
+            op0=ALU.mult, op1=ALU.add,
+        )
+        rstd_hn = rstd_of(1, sq_sums[:, 1, 1:2], to_var, first_var[:])
+        gated = keep.tile([P, H_SIZE], F32)
+        for cols in half:
+            nc.vector.scalar_tensor_tensor(
+                out=gated[:, cols],
+                in0=pre[:, 1, cols],
+                scalar=neg_mean[:, 1:2],
+                in1=r_sb[:, cols],
                 op0=ALU.add,
                 op1=ALU.mult,
             )
+        state_term(half[1])
+        i_n = keep.tile([P, H_SIZE], F32)
+        for cols in half:
             nc.scalar.activation(
-                out=squares[:],
-                in_=pre[:, side, :],
-                func=ACT.Square,
-                bias=neg_mean[:, side : side + 1],
-                scale=1.0,
-                accum_out=sq_sum[:, side : side + 1],
-            )
-            if side == 1:
-                for j in range(HALVES):
-                    nc.vector.scalar_tensor_tensor(
-                        out=gated[:, N_TILE * j : N_TILE * (j + 1)],
-                        in0=pre[:, 1, N_TILE * j : N_TILE * (j + 1)],
-                        scalar=neg_mean[:, 1:2],
-                        in1=r_sb[:, N_TILE * j : N_TILE * (j + 1)],
-                        op0=ALU.add,
-                        op1=ALU.mult,
-                    )
-            nc.gpsimd.tensor_scalar(
-                out=var_eps[:, side : side + 1],
-                in0=sq_sum[:, side : side + 1],
-                scalar1=1.0 / H_SIZE,
-                scalar2=EPS,
-                op0=ALU.mult,
-                op1=ALU.add,
-            )
-            nc.gpsimd.tensor_tensor(
-                out=rstd[:, side : side + 1], in0=var_eps[:, side : side + 1], in1=minus_half[:], op=ALU.pow
+                out=i_n[:, cols], in_=pre[:, 0, cols], func=ACT.Identity, bias=shift[:], scale=rstd_in
             )
 
-        i_n = keep.tile([P, H_SIZE], F32)
-        nc.vector.tensor_scalar(
-            out=i_n[:],
-            in0=pre[:, 0, :],
-            scalar1=neg_mean[:, 0:1],
-            scalar2=rstd[:, 0:1],
-            op0=ALU.add,
-            op1=ALU.mult,
-        )
         arg = keep.tile([P, H_SIZE], F32)
         cand = keep.tile([P, H_SIZE], F32)
+        part = keep.tile([P, H_SIZE], F32)
         res = keep.tile([P, H_SIZE], F32)
-        for j in range(HALVES):
-            cols = slice(N_TILE * j, N_TILE * (j + 1))
+        for cols in thirds:
             nc.vector.scalar_tensor_tensor(
-                out=arg[:, cols], in0=gated[:, cols], scalar=rstd[:, 1:2], in1=i_n[:, cols],
+                out=arg[:, cols], in0=gated[:, cols], scalar=rstd_hn, in1=i_n[:, cols],
                 op0=ALU.mult, op1=ALU.add,
             )
             nc.scalar.activation(out=cand[:, cols], in_=arg[:, cols], func=ACT.Tanh)
-        for j in range(HALVES):
-            cols = slice(N_TILE * j, N_TILE * (j + 1))
-            nc.vector.tensor_tensor(out=res[:, cols], in0=cand[:, cols], in1=one_minus_z[:, cols], op=ALU.mult)
-            nc.vector.tensor_tensor(out=res[:, cols], in0=res[:, cols], in1=z_times_h[:, cols], op=ALU.add)
+
+        def blend(cols):
+            nc.vector.scalar_tensor_tensor(
+                out=part[:, cols], in0=z_sb[:, cols], scalar=-1.0, in1=cand[:, cols],
+                op0=ALU.add, op1=ALU.mult,
+            )
+
+        def finish(cols):
+            nc.vector.tensor_tensor(out=res[:, cols], in0=z_times_h[:, cols], in1=part[:, cols], op=ALU.subtract)
             nc.sync.dma_start(out=out[:, cols], in_=res[:, cols])
+
+        blend(thirds[0])
+        blend(thirds[1])
+        finish(thirds[0])
+        blend(thirds[2])
+        finish(thirds[1])
+        finish(thirds[2])

@@ -181,45 +181,26 @@ def tile_layernormgrucell_pb_s_kernel(
         acc_hn = [product(1, cols) for cols in half]
 
         z_times_h = keep.tile([P, H_SIZE], F32)
+        for cols in half:
+            nc.gpsimd.tensor_tensor(out=z_times_h[:, cols], in0=z_sb[:, cols], in1=h_sb[:, cols], op=ALU.mult)
 
-        def state_term(cols):
-            nc.vector.tensor_tensor(out=z_times_h[:, cols], in0=z_sb[:, cols], in1=h_sb[:, cols], op=ALU.mult)
+        def statistics(side):
+            negative_mean(side)
+            nc.scalar.activation(
+                out=squares[:, side, :], in_=pre[:, side, :], func=ACT.Square,
+                bias=neg_mean[:, side : side + 1], scale=1.0, accum_out=sq_sums[:, side, 0:1],
+            )
+            return rstd_of(side, sq_sums[:, side, 0:1], 1.0 / H_SIZE, EPS)
 
         add_bias(0, 0, acc_in[0])
         add_bias(0, 1, acc_in[1])
-        negative_mean(0)
-        nc.scalar.activation(
-            out=squares[:, 0, :], in_=pre[:, 0, :], func=ACT.Square, bias=neg_mean[:, 0:1], scale=1.0,
-            accum_out=sq_sums[:, 0, 0:1],
-        )
-        rstd_in = rstd_of(0, sq_sums[:, 0, 0:1], 1.0 / H_SIZE, EPS)
+        rstd_in = statistics(0)
         shift = keep.tile([P, 1], F32)
         nc.gpsimd.tensor_scalar(out=shift[:], in0=neg_mean[:, 0:1], scalar1=rstd_in, scalar2=None, op0=ALU.mult)
 
-        to_var = 1.0 / (N_TILE * N_TILE * H_SIZE)
-        for j in range(HALVES):
-            add_bias(1, j, acc_hn[j])
-            nc.scalar.activation(
-                out=squares[:, 1, half[j]], in_=pre[:, 1, half[j]], func=ACT.Square,
-                bias=sums[:, 1, j : j + 1], scale=-float(N_TILE), accum_out=sq_sums[:, 1, j : j + 1],
-            )
-        state_term(half[0])
-        between = keep.tile([P, 2], F32)
-        nc.vector.tensor_scalar(
-            out=between[:, 0:1], in0=sums[:, 1, 0:1], scalar1=sums[:, 1, 1:2], scalar2=1.0 / H_SIZE,
-            op0=ALU.subtract, op1=ALU.mult,
-        )
-        negative_mean(1)
-        nc.vector.tensor_scalar(
-            out=between[:, 1:2], in0=between[:, 0:1], scalar1=between[:, 0:1], scalar2=EPS,
-            op0=ALU.mult, op1=ALU.add,
-        )
-        first_var = keep.tile([P, 1], F32)
-        nc.gpsimd.tensor_scalar(
-            out=first_var[:], in0=sq_sums[:, 1, 0:1], scalar1=to_var, scalar2=between[:, 1:2],
-            op0=ALU.mult, op1=ALU.add,
-        )
-        rstd_hn = rstd_of(1, sq_sums[:, 1, 1:2], to_var, first_var[:])
+        add_bias(1, 0, acc_hn[0])
+        add_bias(1, 1, acc_hn[1])
+        rstd_hn = statistics(1)
         gated = keep.tile([P, H_SIZE], F32)
         for cols in half:
             nc.vector.scalar_tensor_tensor(
@@ -230,7 +211,6 @@ def tile_layernormgrucell_pb_s_kernel(
                 op0=ALU.add,
                 op1=ALU.mult,
             )
-        state_term(half[1])
         i_n = keep.tile([P, H_SIZE], F32)
         for cols in half:
             nc.scalar.activation(

@@ -24,6 +24,7 @@ WORDS = K_PASS // 2
 N_TILE = 512
 HALVES = H_SIZE // N_TILE
 BIAS_WORDS = H_SIZE // 2 // P
+WARM_UPS = 14
 QUADRANTS = 4
 
 FLOPS = 2 * P * (I_SIZE + H_SIZE) * H_SIZE
@@ -37,6 +38,9 @@ def tile_layernormgrucell_pb_s_kernel(
         keep = ctx.enter_context(tc.tile_pool(name="keep", bufs=1))
         psum = ctx.enter_context(tc.psum_pool(name="psum", bufs=8))
         ctx.enter_context(tc.manual_schedule())
+
+        idle = keep.tile([P, P], F32)
+        nc.vector.memset(idle[:], 0.0)
 
         x_sb = keep.tile([P, I_SIZE], BF16)
         h_sb = keep.tile([P, H_SIZE], BF16)
@@ -93,6 +97,10 @@ def tile_layernormgrucell_pb_s_kernel(
             nc.vector.quantize_mx(
                 out=a_codes[:, c, :].bitcast(FP8X4), scales=a_scales[:, c, :], in_=grouped[:, c, :]
             )
+
+        unread = psum.tile([P, 4, P], F32, tag="bank")
+        for i in range(WARM_UPS):
+            nc.tensor.transpose(unread[:, i % 4, :], idle[:], idle[:])
 
         for c in range(PASSES):
             flipped = psum.tile([P, 2, P], F32, tag="bank")

@@ -48,8 +48,8 @@ def tile_layernormgrucell_pb_s_kernel(
         nc.scalar.dma_start(out=h_sb[:], in_=h)
 
         warm = keep.tile([P, 1], F32)
-        nc.vector.memset(warm[:], 0.0)
-        nc.scalar.activation(out=warm[:], in_=warm[:], func=ACT.Tanh)
+        nc.vector.memset(warm[:], 1.0)
+        nc.scalar.activation(out=warm[:], in_=warm[:], func=ACT.Abs_reciprocal_sqrt)
 
         w_words = keep.tile([P, PASSES, 2 * H_SIZE], U8, align_bytes=64)
         w_scales = keep.tile([P, PASSES, H_SIZE], U8, align_bytes=64)
@@ -81,8 +81,8 @@ def tile_layernormgrucell_pb_s_kernel(
         r_sb = keep.tile([P, H_SIZE], BF16)
         nc.gpsimd.dma_start(out=z_sb[:], in_=z)
         nc.gpsimd.dma_start(out=r_sb[:], in_=r)
-        minus_half = keep.tile([P, 1], F32)
-        nc.gpsimd.memset(minus_half[:], -0.5)
+        eps = keep.tile([P, 1], F32)
+        nc.vector.tensor_scalar(out=eps[:], in0=idle[:, 0:1], scalar1=0.0, scalar2=EPS, op0=ALU.mult, op1=ALU.add)
 
         grouped = keep.tile([P, PASSES, P * PACK], BF16, align_bytes=64)
         a_codes = keep.tile([P, PASSES, P], U32, align_bytes=64)
@@ -162,15 +162,6 @@ def tile_layernormgrucell_pb_s_kernel(
                 accum_out=sums[:, side, i : i + 1],
             )
 
-        def rstd_of(side, square_sum, mean_square_scale, rest):
-            tiny = keep.tile([P, 2], F32, tag=f"tiny{side}")
-            nc.gpsimd.tensor_scalar(
-                out=tiny[:, 0:1], in0=square_sum, scalar1=mean_square_scale, scalar2=rest,
-                op0=ALU.mult, op1=ALU.add,
-            )
-            nc.gpsimd.tensor_tensor(out=tiny[:, 1:2], in0=tiny[:, 0:1], in1=minus_half[:], op=ALU.pow)
-            return tiny[:, 1:2]
-
         def negative_mean(side):
             nc.vector.tensor_scalar(
                 out=neg_mean[:, side : side + 1], in0=sums[:, side, 0:1], scalar1=sums[:, side, 1:2],
@@ -189,28 +180,33 @@ def tile_layernormgrucell_pb_s_kernel(
         acc_hn = [product(1, cols) for cols in half]
 
         z_times_h = keep.tile([P, H_SIZE], F32)
-        for cols in half:
-            nc.gpsimd.tensor_tensor(out=z_times_h[:, cols], in0=z_sb[:, cols], in1=h_sb[:, cols], op=ALU.mult)
+        nc.gpsimd.tensor_tensor(
+            out=z_times_h[:, half[0]], in0=z_sb[:, half[0]], in1=h_sb[:, half[0]], op=ALU.mult
+        )
 
-        def statistics(side):
+        def square_deviations(side):
             negative_mean(side)
             nc.scalar.activation(
                 out=squares[:, side, :], in_=pre[:, side, :], func=ACT.Square,
                 bias=neg_mean[:, side : side + 1], scale=1.0, accum_out=sq_sums[:, side, 0:1],
             )
-            return rstd_of(side, sq_sums[:, side, 0:1], 1.0 / H_SIZE, EPS)
 
+        scale_in = keep.tile([P, 1], F32)
+        ratio = keep.tile([P, 1], F32)
+        to_ratio = keep.tile([P, 2], F32)
         add_bias(0, 0, acc_in[0])
         add_bias(0, 1, acc_in[1])
-        rstd_in = statistics(0)
-        shift = keep.tile([P, 1], F32)
-        nc.gpsimd.tensor_scalar(out=shift[:], in0=neg_mean[:, 0:1], scalar1=rstd_in, scalar2=None, op0=ALU.mult)
+        square_deviations(0)
+        nc.scalar.activation(
+            out=scale_in[:], in_=sq_sums[:, 0, 0:1], func=ACT.Abs_reciprocal_sqrt, scale=1.0 / H_SIZE, bias=eps[:]
+        )
 
         add_bias(1, 0, acc_hn[0])
         add_bias(1, 1, acc_hn[1])
-        rstd_hn = statistics(1)
+        square_deviations(1)
         gated = keep.tile([P, H_SIZE], F32)
-        for cols in half:
+
+        def gate(cols):
             nc.vector.scalar_tensor_tensor(
                 out=gated[:, cols],
                 in0=pre[:, 1, cols],
@@ -219,22 +215,38 @@ def tile_layernormgrucell_pb_s_kernel(
                 op0=ALU.add,
                 op1=ALU.mult,
             )
-        i_n = keep.tile([P, H_SIZE], F32)
-        for cols in half:
-            nc.scalar.activation(
-                out=i_n[:, cols], in_=pre[:, 0, cols], func=ACT.Identity, bias=shift[:], scale=rstd_in
-            )
 
+        nc.vector.tensor_scalar(
+            out=to_ratio[:, 0:1], in0=scale_in[:], scalar1=scale_in[:], scalar2=1.0 / H_SIZE,
+            op0=ALU.mult, op1=ALU.mult,
+        )
+        gate(half[0])
+        nc.vector.tensor_scalar(
+            out=to_ratio[:, 1:2], in0=to_ratio[:, 0:1], scalar1=EPS * H_SIZE, scalar2=None, op0=ALU.mult
+        )
+        gate(half[1])
+        nc.scalar.activation(
+            out=ratio[:], in_=sq_sums[:, 1, 0:1], func=ACT.Abs_reciprocal_sqrt,
+            scale=to_ratio[:, 0:1], bias=to_ratio[:, 1:2],
+        )
+        nc.scalar.activation(out=warm[:], in_=warm[:], func=ACT.Tanh)
+
+        shift = keep.tile([P, 1], F32)
         arg = keep.tile([P, H_SIZE], F32)
         cand = keep.tile([P, H_SIZE], F32)
         part = keep.tile([P, H_SIZE], F32)
         res = keep.tile([P, H_SIZE], F32)
+        nc.vector.tensor_scalar(
+            out=shift[:], in0=neg_mean[:, 0:1], scalar1=scale_in[:], scalar2=None, op0=ALU.mult
+        )
         for cols in thirds:
             nc.vector.scalar_tensor_tensor(
-                out=arg[:, cols], in0=gated[:, cols], scalar=rstd_hn, in1=i_n[:, cols],
+                out=arg[:, cols], in0=gated[:, cols], scalar=ratio[:], in1=pre[:, 0, cols],
                 op0=ALU.mult, op1=ALU.add,
             )
-            nc.scalar.activation(out=cand[:, cols], in_=arg[:, cols], func=ACT.Tanh)
+            nc.scalar.activation(
+                out=cand[:, cols], in_=arg[:, cols], func=ACT.Tanh, bias=shift[:], scale=scale_in[:]
+            )
 
         def blend(cols):
             nc.vector.scalar_tensor_tensor(
@@ -246,6 +258,9 @@ def tile_layernormgrucell_pb_s_kernel(
             nc.vector.tensor_tensor(out=res[:, cols], in0=z_times_h[:, cols], in1=part[:, cols], op=ALU.subtract)
             nc.sync.dma_start(out=out[:, cols], in_=res[:, cols])
 
+        nc.vector.tensor_tensor(
+            out=z_times_h[:, half[1]], in0=z_sb[:, half[1]], in1=h_sb[:, half[1]], op=ALU.mult
+        )
         blend(thirds[0])
         blend(thirds[1])
         finish(thirds[0])

@@ -24,7 +24,9 @@ WORDS = K_PASS // 2
 N_TILE = 512
 HALVES = H_SIZE // N_TILE
 BIAS_WORDS = H_SIZE // 2 // P
-WARM_UPS = 14
+WARM_UPS = 10
+TO_VAR = 1.0 / (N_TILE * N_TILE * H_SIZE)
+HALF_DISTANCE = 16.0
 QUADRANTS = 4
 
 FLOPS = 2 * P * (I_SIZE + H_SIZE) * H_SIZE
@@ -44,6 +46,10 @@ def tile_layernormgrucell_pb_s_kernel(
 
         x_sb = keep.tile([P, I_SIZE], BF16)
         h_sb = keep.tile([P, H_SIZE], BF16)
+        b_in_words = keep.tile([P, BIAS_WORDS * 2], BF16)
+        b_hn_words = keep.tile([P, BIAS_WORDS * 2], BF16)
+        nc.scalar.dma_start(out=b_in_words[:], in_=b_in.rearrange("(w e) -> w e", w=P))
+        nc.gpsimd.dma_start(out=b_hn_words[:], in_=b_hn.rearrange("(w e) -> w e", w=P))
         nc.scalar.dma_start(out=x_sb[:], in_=x)
         nc.scalar.dma_start(out=h_sb[:], in_=h)
 
@@ -71,18 +77,12 @@ def tile_layernormgrucell_pb_s_kernel(
                 in_=W_hn_scales[:, 4 * q : 4 * q + 4, :].bitcast(I32).rearrange("g s n -> s g n"),
             )
 
-        b_in_words = keep.tile([P, BIAS_WORDS * 2], BF16)
-        b_hn_words = keep.tile([P, BIAS_WORDS * 2], BF16)
-        nc.gpsimd.dma_start(out=b_in_words[:], in_=b_in.rearrange("(w e) -> w e", w=P))
         ident = keep.tile([P, P], F32)
         make_identity(nc, ident[:])
-        nc.gpsimd.dma_start(out=b_hn_words[:], in_=b_hn.rearrange("(w e) -> w e", w=P))
         z_sb = keep.tile([P, H_SIZE], BF16)
         r_sb = keep.tile([P, H_SIZE], BF16)
         nc.gpsimd.dma_start(out=z_sb[:], in_=z)
         nc.gpsimd.dma_start(out=r_sb[:], in_=r)
-        eps = keep.tile([P, 1], F32)
-        nc.vector.tensor_scalar(out=eps[:], in0=idle[:, 0:1], scalar1=0.0, scalar2=EPS, op0=ALU.mult, op1=ALU.add)
 
         grouped = keep.tile([P, PASSES, P * PACK], BF16, align_bytes=64)
         a_codes = keep.tile([P, PASSES, P], U32, align_bytes=64)
@@ -162,72 +162,84 @@ def tile_layernormgrucell_pb_s_kernel(
                 accum_out=sums[:, side, i : i + 1],
             )
 
-        def negative_mean(side):
-            nc.vector.tensor_scalar(
-                out=neg_mean[:, side : side + 1], in0=sums[:, side, 0:1], scalar1=sums[:, side, 1:2],
-                scalar2=-1.0 / H_SIZE, op0=ALU.add, op1=ALU.mult,
-            )
-            return neg_mean[:, side : side + 1]
-
         half = [slice(0, N_TILE), slice(N_TILE, H_SIZE)]
         thirds = [slice(0, 512), slice(512, 768), slice(768, 1024)]
         pieces = [half, half]
-        neg_mean = keep.tile([P, 2], F32)
 
         spread_bias(0, b_in_words)
-        acc_in = [product(0, cols) for cols in half]
         spread_bias(1, b_hn_words)
+        acc_in = [product(0, cols) for cols in half]
         acc_hn = [product(1, cols) for cols in half]
 
-        z_times_h = keep.tile([P, H_SIZE], F32)
-        nc.gpsimd.tensor_tensor(
-            out=z_times_h[:, half[0]], in0=z_sb[:, half[0]], in1=h_sb[:, half[0]], op=ALU.mult
-        )
-
-        def square_deviations(side):
-            negative_mean(side)
+        def square_deviations(side, j):
             nc.scalar.activation(
-                out=squares[:, side, :], in_=pre[:, side, :], func=ACT.Square,
-                bias=neg_mean[:, side : side + 1], scale=1.0, accum_out=sq_sums[:, side, 0:1],
+                out=squares[:, side, half[j]], in_=pre[:, side, half[j]], func=ACT.Square,
+                bias=sums[:, side, j : j + 1], scale=-float(N_TILE), accum_out=sq_sums[:, side, j : j + 1],
+            )
+
+        def negative_mean(engine, out, side):
+            engine.tensor_scalar(
+                out=out, in0=sums[:, side, 0:1], scalar1=sums[:, side, 1:2], scalar2=-1.0 / H_SIZE,
+                op0=ALU.add, op1=ALU.mult,
             )
 
         scale_in = keep.tile([P, 1], F32)
         ratio = keep.tile([P, 1], F32)
-        to_ratio = keep.tile([P, 2], F32)
-        add_bias(0, 0, acc_in[0])
-        add_bias(0, 1, acc_in[1])
-        square_deviations(0)
-        nc.scalar.activation(
-            out=scale_in[:], in_=sq_sums[:, 0, 0:1], func=ACT.Abs_reciprocal_sqrt, scale=1.0 / H_SIZE, bias=eps[:]
-        )
+        for j in range(HALVES):
+            add_bias(0, j, acc_in[j])
+            square_deviations(0, j)
 
-        add_bias(1, 0, acc_hn[0])
-        add_bias(1, 1, acc_hn[1])
-        square_deviations(1)
-        gated = keep.tile([P, H_SIZE], F32)
-
-        def gate(cols):
-            nc.vector.scalar_tensor_tensor(
-                out=gated[:, cols],
-                in0=pre[:, 1, cols],
-                scalar=neg_mean[:, 1:2],
-                in1=r_sb[:, cols],
-                op0=ALU.add,
-                op1=ALU.mult,
+        def distance(engine, dist, side):
+            engine.tensor_scalar(
+                out=dist, in0=sums[:, side, 0:1], scalar1=sums[:, side, 1:2], scalar2=HALF_DISTANCE,
+                op0=ALU.subtract, op1=ALU.mult,
             )
 
-        nc.vector.tensor_scalar(
-            out=to_ratio[:, 0:1], in0=scale_in[:], scalar1=scale_in[:], scalar2=1.0 / H_SIZE,
-            op0=ALU.mult, op1=ALU.mult,
+        def distance_squared(engine, rest, dist):
+            engine.tensor_scalar(
+                out=rest, in0=dist, scalar1=dist, scalar2=EPS / TO_VAR, op0=ALU.mult, op1=ALU.add
+            )
+
+        side_0 = keep.tile([P, 4], F32)
+        dist_in, rest_in, bias_in, mean_in = [side_0[:, i : i + 1] for i in range(4)]
+        distance(nc.gpsimd, dist_in, 0)
+        distance_squared(nc.gpsimd, rest_in, dist_in)
+        nc.gpsimd.tensor_scalar(
+            out=bias_in, in0=sq_sums[:, 0, 0:1], scalar1=rest_in, scalar2=TO_VAR, op0=ALU.add, op1=ALU.mult
         )
-        gate(half[0])
-        nc.vector.tensor_scalar(
-            out=to_ratio[:, 1:2], in0=to_ratio[:, 0:1], scalar1=EPS * H_SIZE, scalar2=None, op0=ALU.mult
-        )
-        gate(half[1])
+        negative_mean(nc.gpsimd, mean_in, 0)
+        z_times_h = keep.tile([P, H_SIZE], F32)
+        for cols in [slice(0, 256), slice(256, 512)]:
+            nc.gpsimd.tensor_tensor(out=z_times_h[:, cols], in0=z_sb[:, cols], in1=h_sb[:, cols], op=ALU.mult)
+
+        add_bias(1, 0, acc_hn[0])
+        square_deviations(1, 0)
         nc.scalar.activation(
-            out=ratio[:], in_=sq_sums[:, 1, 0:1], func=ACT.Abs_reciprocal_sqrt,
-            scale=to_ratio[:, 0:1], bias=to_ratio[:, 1:2],
+            out=scale_in[:], in_=sq_sums[:, 0, 1:2], func=ACT.Abs_reciprocal_sqrt, scale=TO_VAR, bias=bias_in
+        )
+        add_bias(1, 1, acc_hn[1])
+        square_deviations(1, 1)
+
+        side_1 = keep.tile([P, 5], F32)
+        dist_hn, rest_hn, mean_hn, to_ratio, bias_hn = [side_1[:, i : i + 1] for i in range(5)]
+        gated = keep.tile([P, H_SIZE], F32)
+
+        distance(nc.vector, dist_hn, 1)
+        negative_mean(nc.vector, mean_hn, 1)
+        nc.vector.tensor_scalar(
+            out=to_ratio, in0=scale_in[:], scalar1=scale_in[:], scalar2=TO_VAR, op0=ALU.mult, op1=ALU.mult
+        )
+        distance_squared(nc.vector, rest_hn, dist_hn)
+        nc.vector.tensor_scalar(
+            out=bias_hn, in0=sq_sums[:, 1, 0:1], scalar1=rest_hn, scalar2=to_ratio, op0=ALU.add, op1=ALU.mult
+        )
+        for cols in half:
+            nc.vector.scalar_tensor_tensor(
+                out=gated[:, cols], in0=pre[:, 1, cols], scalar=mean_hn, in1=r_sb[:, cols],
+                op0=ALU.add, op1=ALU.mult,
+            )
+        nc.scalar.activation(
+            out=ratio[:], in_=sq_sums[:, 1, 1:2], func=ACT.Abs_reciprocal_sqrt, scale=to_ratio, bias=bias_hn
         )
         nc.scalar.activation(out=warm[:], in_=warm[:], func=ACT.Tanh)
 
@@ -237,7 +249,7 @@ def tile_layernormgrucell_pb_s_kernel(
         part = keep.tile([P, H_SIZE], F32)
         res = keep.tile([P, H_SIZE], F32)
         nc.vector.tensor_scalar(
-            out=shift[:], in0=neg_mean[:, 0:1], scalar1=scale_in[:], scalar2=None, op0=ALU.mult
+            out=shift[:], in0=mean_in, scalar1=scale_in[:], scalar2=None, op0=ALU.mult
         )
         for cols in thirds:
             nc.vector.scalar_tensor_tensor(

@@ -41,32 +41,31 @@ def tile_layernormgrucell_pb_s_kernel(
         psum = ctx.enter_context(tc.psum_pool(name="psum", bufs=8))
         ctx.enter_context(tc.manual_schedule())
 
-        idle = keep.tile([P, P], F32)
-        nc.vector.memset(idle[:], 0.0)
-
         x_sb = keep.tile([P, I_SIZE], BF16)
         h_sb = keep.tile([P, H_SIZE], BF16)
         b_in_words = keep.tile([P, BIAS_WORDS * 2], BF16)
         b_hn_words = keep.tile([P, BIAS_WORDS * 2], BF16)
-        nc.scalar.dma_start(out=b_in_words[:], in_=b_in.rearrange("(w e) -> w e", w=P))
         nc.gpsimd.dma_start(out=b_hn_words[:], in_=b_hn.rearrange("(w e) -> w e", w=P))
         nc.scalar.dma_start(out=x_sb[:], in_=x)
+        nc.scalar.dma_start(out=b_in_words[:], in_=b_in.rearrange("(w e) -> w e", w=P))
         nc.scalar.dma_start(out=h_sb[:], in_=h)
 
+        w_scales = keep.tile([P, PASSES, H_SIZE], U8, align_bytes=64)
+        nc.vector.memset(w_scales[:, 0, :].bitcast(I32), 0)
         warm = keep.tile([P, 1], F32)
         nc.vector.memset(warm[:], 1.0)
+        idle = keep.tile([P, P], F32)
+        nc.vector.memset(idle[:], 0.0)
         nc.scalar.activation(out=warm[:], in_=warm[:], func=ACT.Abs_reciprocal_sqrt)
 
         w_words = keep.tile([P, PASSES, 2 * H_SIZE], U8, align_bytes=64)
-        w_scales = keep.tile([P, PASSES, H_SIZE], U8, align_bytes=64)
-        nc.vector.memset(w_scales[:, 0, :].bitcast(I32), 0)
         nc.vector.memset(w_scales[:, 1:PASSES, :].bitcast(I32), 0)
-        nc.sync.dma_start(out=w_words[:, 0, :].bitcast(I32), in_=W_in_words[0].bitcast(I32))
         for q in range(QUADRANTS):
             nc.sync.dma_start(
                 out=w_scales[32 * q : 32 * q + 4, 0, :].bitcast(I32),
                 in_=W_in_scales[0, 4 * q : 4 * q + 4, :].bitcast(I32),
             )
+        nc.sync.dma_start(out=w_words[:, 0, :].bitcast(I32), in_=W_in_words[0].bitcast(I32))
         nc.sync.dma_start(
             out=w_words[:, 1:PASSES, :].bitcast(I32),
             in_=W_hn_words.bitcast(I32).rearrange("g p n -> p g n"),
@@ -93,6 +92,22 @@ def tile_layernormgrucell_pb_s_kernel(
             h_sb[:].bitcast(F32)[:, WORDS : 2 * WORDS],
         ]
 
+        bias = keep.tile([P, 2, H_SIZE], BF16)
+
+        def spread_bias(bias_words):
+            spread = psum.tile([P, BIAS_WORDS, P], F32, tag="bank")
+            for m in range(BIAS_WORDS):
+                nc.tensor.transpose(
+                    spread[:, m, :], bias_words[:].bitcast(F32)[:, m : m + 1].to_broadcast([P, P]), ident[:]
+                )
+            return spread
+
+        def collect_bias(side, spread):
+            nc.scalar.copy(
+                out=bias[:, side, :].bitcast(F32).rearrange("p (w m) -> p w m", m=BIAS_WORDS),
+                in_=spread[:].rearrange("p m w -> p w m"),
+            )
+
         def quantise(c):
             nc.vector.quantize_mx(
                 out=a_codes[:, c, :].bitcast(FP8X4), scales=a_scales[:, c, :], in_=grouped[:, c, :]
@@ -113,21 +128,10 @@ def tile_layernormgrucell_pb_s_kernel(
                 nc.scalar.copy(out=side_by_side, in_=flipped[:].rearrange("p u b -> p b u"))
             if c == 0:
                 quantise(0)
+                spread_in = spread_bias(b_in_words)
+        collect_bias(0, spread_in)
         quantise(1)
         quantise(2)
-
-        bias = keep.tile([P, 2, H_SIZE], BF16)
-
-        def spread_bias(side, bias_words):
-            spread = psum.tile([P, BIAS_WORDS, P], F32, tag="bank")
-            for m in range(BIAS_WORDS):
-                nc.tensor.transpose(
-                    spread[:, m, :], bias_words[:].bitcast(F32)[:, m : m + 1].to_broadcast([P, P]), ident[:]
-                )
-            nc.scalar.copy(
-                out=bias[:, side, :].bitcast(F32).rearrange("p (w m) -> p w m", m=BIAS_WORDS),
-                in_=spread[:].rearrange("p m w -> p w m"),
-            )
 
         passes_of_side = [[0], [1, 2]]
         pre = keep.tile([P, 2, H_SIZE], F32)
@@ -166,9 +170,8 @@ def tile_layernormgrucell_pb_s_kernel(
         thirds = [slice(0, 512), slice(512, 768), slice(768, 1024)]
         pieces = [half, half]
 
-        spread_bias(0, b_in_words)
-        spread_bias(1, b_hn_words)
         acc_in = [product(0, cols) for cols in half]
+        collect_bias(1, spread_bias(b_hn_words))
         acc_hn = [product(1, cols) for cols in half]
 
         def square_deviations(side, j):
@@ -251,7 +254,7 @@ def tile_layernormgrucell_pb_s_kernel(
         nc.vector.tensor_scalar(
             out=shift[:], in0=mean_in, scalar1=scale_in[:], scalar2=None, op0=ALU.mult
         )
-        for cols in thirds:
+        for cols in half:
             nc.vector.scalar_tensor_tensor(
                 out=arg[:, cols], in0=gated[:, cols], scalar=ratio[:], in1=pre[:, 0, cols],
                 op0=ALU.mult, op1=ALU.add,

@@ -24,7 +24,7 @@ WORDS = K_PASS // 2
 N_TILE = 512
 HALVES = H_SIZE // N_TILE
 BIAS_WORDS = H_SIZE // 2 // P
-WARM_UPS = 10
+WARM_UPS = 6
 TO_VAR = 1.0 / (N_TILE * N_TILE * H_SIZE)
 HALF_DISTANCE = 16.0
 QUADRANTS = 4
@@ -46,8 +46,8 @@ def tile_layernormgrucell_pb_s_kernel(
         b_in_words = keep.tile([P, BIAS_WORDS * 2], BF16)
         b_hn_words = keep.tile([P, BIAS_WORDS * 2], BF16)
         nc.gpsimd.dma_start(out=b_hn_words[:], in_=b_hn.rearrange("(w e) -> w e", w=P))
-        nc.scalar.dma_start(out=x_sb[:], in_=x)
         nc.scalar.dma_start(out=b_in_words[:], in_=b_in.rearrange("(w e) -> w e", w=P))
+        nc.scalar.dma_start(out=x_sb[:], in_=x)
         nc.scalar.dma_start(out=h_sb[:], in_=h)
 
         w_scales = keep.tile([P, PASSES, H_SIZE], U8, align_bytes=64)
@@ -167,7 +167,7 @@ def tile_layernormgrucell_pb_s_kernel(
             )
 
         half = [slice(0, N_TILE), slice(N_TILE, H_SIZE)]
-        thirds = [slice(0, 512), slice(512, 768), slice(768, 1024)]
+        quarters = [slice(c, c + 256) for c in range(0, H_SIZE, 256)]
         pieces = [half, half]
 
         acc_in = [product(0, cols) for cols in half]
@@ -203,6 +203,12 @@ def tile_layernormgrucell_pb_s_kernel(
                 out=rest, in0=dist, scalar1=dist, scalar2=EPS / TO_VAR, op0=ALU.mult, op1=ALU.add
             )
 
+        z_times_h = keep.tile([P, H_SIZE], F32)
+
+        def state_term(engine, cols):
+            engine.tensor_tensor(out=z_times_h[:, cols], in0=z_sb[:, cols], in1=h_sb[:, cols], op=ALU.mult)
+
+        state_term(nc.gpsimd, quarters[0])
         side_0 = keep.tile([P, 4], F32)
         dist_in, rest_in, bias_in, mean_in = [side_0[:, i : i + 1] for i in range(4)]
         distance(nc.gpsimd, dist_in, 0)
@@ -211,9 +217,8 @@ def tile_layernormgrucell_pb_s_kernel(
             out=bias_in, in0=sq_sums[:, 0, 0:1], scalar1=rest_in, scalar2=TO_VAR, op0=ALU.add, op1=ALU.mult
         )
         negative_mean(nc.gpsimd, mean_in, 0)
-        z_times_h = keep.tile([P, H_SIZE], F32)
-        for cols in [slice(0, 256), slice(256, 512)]:
-            nc.gpsimd.tensor_tensor(out=z_times_h[:, cols], in0=z_sb[:, cols], in1=h_sb[:, cols], op=ALU.mult)
+        state_term(nc.gpsimd, quarters[1])
+        state_term(nc.gpsimd, quarters[2])
 
         add_bias(1, 0, acc_hn[0])
         square_deviations(1, 0)
@@ -259,6 +264,9 @@ def tile_layernormgrucell_pb_s_kernel(
                 out=arg[:, cols], in0=gated[:, cols], scalar=ratio[:], in1=pre[:, 0, cols],
                 op0=ALU.mult, op1=ALU.add,
             )
+
+        state_term(nc.vector, quarters[3])
+        for cols in quarters:
             nc.scalar.activation(
                 out=cand[:, cols], in_=arg[:, cols], func=ACT.Tanh, bias=shift[:], scale=scale_in[:]
             )
@@ -271,14 +279,18 @@ def tile_layernormgrucell_pb_s_kernel(
 
         def finish(cols):
             nc.vector.tensor_tensor(out=res[:, cols], in0=z_times_h[:, cols], in1=part[:, cols], op=ALU.subtract)
+
+        def store(cols):
             nc.sync.dma_start(out=out[:, cols], in_=res[:, cols])
 
-        nc.vector.tensor_tensor(
-            out=z_times_h[:, half[1]], in0=z_sb[:, half[1]], in1=h_sb[:, half[1]], op=ALU.mult
-        )
-        blend(thirds[0])
-        blend(thirds[1])
-        finish(thirds[0])
-        blend(thirds[2])
-        finish(thirds[1])
-        finish(thirds[2])
+        blend(quarters[0])
+        blend(quarters[1])
+        finish(quarters[0])
+        blend(quarters[2])
+        finish(quarters[1])
+        store(half[0])
+        blend(quarters[3])
+        finish(quarters[2])
+        store(quarters[2])
+        finish(quarters[3])
+        store(quarters[3])

@@ -24,7 +24,7 @@ WORDS = K_PASS // 2
 N_TILE = 512
 HALVES = H_SIZE // N_TILE
 BIAS_WORDS = H_SIZE // 2 // P
-WARM_UPS = 6
+WARM_UPS = 4
 TO_VAR = 1.0 / (N_TILE * N_TILE * H_SIZE)
 HALF_DISTANCE = 16.0
 QUADRANTS = 4
@@ -38,7 +38,7 @@ def tile_layernormgrucell_pb_s_kernel(
     nc = tc.nc
     with ExitStack() as ctx:
         keep = ctx.enter_context(tc.tile_pool(name="keep", bufs=1))
-        psum = ctx.enter_context(tc.psum_pool(name="psum", bufs=8))
+        psum = ctx.enter_context(tc.psum_pool(name="psum", bufs=7))
         ctx.enter_context(tc.manual_schedule())
 
         x_sb = keep.tile([P, I_SIZE], BF16)
@@ -113,9 +113,13 @@ def tile_layernormgrucell_pb_s_kernel(
                 out=a_codes[:, c, :].bitcast(FP8X4), scales=a_scales[:, c, :], in_=grouped[:, c, :]
             )
 
-        unread = psum.tile([P, 4, P], F32, tag="bank")
+        unread = psum.tile([P, 4, P], F32, tag="unread", bufs=1)
+
+        def keep_warm(i):
+            nc.tensor.matmul(unread[:, i % 4, :], lhsT=idle[:], rhs=idle[:], start=True, stop=True)
+
         for i in range(WARM_UPS):
-            nc.tensor.transpose(unread[:, i % 4, :], idle[:], idle[:])
+            keep_warm(i)
 
         for c in range(PASSES):
             flipped = psum.tile([P, 2, P], F32, tag="bank")
@@ -128,7 +132,10 @@ def tile_layernormgrucell_pb_s_kernel(
                 nc.scalar.copy(out=side_by_side, in_=flipped[:].rearrange("p u b -> p b u"))
             if c == 0:
                 quantise(0)
+                keep_warm(0)
                 spread_in = spread_bias(b_in_words)
+                keep_warm(1)
+        keep_warm(2)
         collect_bias(0, spread_in)
         quantise(1)
         quantise(2)

@@ -41,6 +41,8 @@ def tile_layernormgrucell_pb_s_kernel(
         psum = ctx.enter_context(tc.psum_pool(name="psum", bufs=7))
         ctx.enter_context(tc.manual_schedule())
 
+        idle = keep.tile([P, P], F32)
+        nc.gpsimd.memset(idle[:], 0.0)
         x_sb = keep.tile([P, I_SIZE], BF16)
         h_sb = keep.tile([P, H_SIZE], BF16)
         b_in_words = keep.tile([P, BIAS_WORDS * 2], BF16)
@@ -54,8 +56,6 @@ def tile_layernormgrucell_pb_s_kernel(
         nc.vector.memset(w_scales[:, 0, :].bitcast(I32), 0)
         warm = keep.tile([P, 1], F32)
         nc.vector.memset(warm[:], 1.0)
-        idle = keep.tile([P, P], F32)
-        nc.vector.memset(idle[:], 0.0)
         nc.scalar.activation(out=warm[:], in_=warm[:], func=ACT.Abs_reciprocal_sqrt)
 
         w_words = keep.tile([P, PASSES, 2 * H_SIZE], U8, align_bytes=64)

@@ -47,25 +47,21 @@ def tile_layernormgrucell_pb_s_kernel(
         h_sb = keep.tile([P, H_SIZE], BF16)
         b_in_words = keep.tile([P, BIAS_WORDS * 2], BF16)
         b_hn_words = keep.tile([P, BIAS_WORDS * 2], BF16)
-        nc.gpsimd.dma_start(out=b_hn_words[:], in_=b_hn.rearrange("(w e) -> w e", w=P))
-        nc.scalar.dma_start(out=b_in_words[:], in_=b_in.rearrange("(w e) -> w e", w=P))
-        nc.scalar.dma_start(out=x_sb[:], in_=x)
-        nc.scalar.dma_start(out=h_sb[:], in_=h)
-
         w_scales = keep.tile([P, PASSES, H_SIZE], U8, align_bytes=64)
         nc.vector.memset(w_scales[:, 0, :].bitcast(I32), 0)
-        warm = keep.tile([P, 1], F32)
-        nc.vector.memset(warm[:], 1.0)
-        nc.scalar.activation(out=warm[:], in_=warm[:], func=ACT.Abs_reciprocal_sqrt)
+        nc.gpsimd.dma_start(out=b_hn_words[:], in_=b_hn.rearrange("(w e) -> w e", w=P))
 
         w_words = keep.tile([P, PASSES, 2 * H_SIZE], U8, align_bytes=64)
-        nc.vector.memset(w_scales[:, 1:PASSES, :].bitcast(I32), 0)
+        nc.scalar.dma_start(out=b_in_words[:], in_=b_in.rearrange("(w e) -> w e", w=P))
         for q in range(QUADRANTS):
             nc.sync.dma_start(
                 out=w_scales[32 * q : 32 * q + 4, 0, :].bitcast(I32),
                 in_=W_in_scales[0, 4 * q : 4 * q + 4, :].bitcast(I32),
             )
+        nc.scalar.dma_start(out=x_sb[:], in_=x)
+        nc.scalar.dma_start(out=h_sb[:], in_=h)
         nc.sync.dma_start(out=w_words[:, 0, :].bitcast(I32), in_=W_in_words[0].bitcast(I32))
+        nc.vector.memset(w_scales[:, 1:PASSES, :].bitcast(I32), 0)
         nc.sync.dma_start(
             out=w_words[:, 1:PASSES, :].bitcast(I32),
             in_=W_hn_words.bitcast(I32).rearrange("g p n -> p g n"),
@@ -75,6 +71,10 @@ def tile_layernormgrucell_pb_s_kernel(
                 out=w_scales[32 * q : 32 * q + 4, 1:PASSES, :].bitcast(I32),
                 in_=W_hn_scales[:, 4 * q : 4 * q + 4, :].bitcast(I32).rearrange("g s n -> s g n"),
             )
+
+        warm = keep.tile([P, 1], F32)
+        nc.vector.memset(warm[:], 1.0)
+        nc.scalar.activation(out=warm[:], in_=warm[:], func=ACT.Abs_reciprocal_sqrt)
 
         ident = keep.tile([P, P], F32)
         make_identity(nc, ident[:])
@@ -132,10 +132,8 @@ def tile_layernormgrucell_pb_s_kernel(
                 nc.scalar.copy(out=side_by_side, in_=flipped[:].rearrange("p u b -> p b u"))
             if c == 0:
                 quantise(0)
-                keep_warm(0)
                 spread_in = spread_bias(b_in_words)
-                keep_warm(1)
-        keep_warm(2)
+        keep_warm(0)
         collect_bias(0, spread_in)
         quantise(1)
         quantise(2)

from contextlib import ExitStack

import concourse.mybir as mybir
from concourse.masks import make_identity

F32 = mybir.dt.float32
BF16 = mybir.dt.bfloat16
I32 = mybir.dt.int32
U32 = mybir.dt.uint32
U8 = mybir.dt.uint8
FP8X4 = mybir.dt.float8_e4m3fn_x4
FP4X4 = mybir.dt.float4_e2m1fn_x4
ALU = mybir.AluOpType
ACT = mybir.ActivationFunctionType

P = 128
I_SIZE = 512
H_SIZE = 1024
EPS = 1e-5
PACK = 4
K_PASS = P * PACK
PASSES = (I_SIZE + H_SIZE) // K_PASS
WORDS = K_PASS // 2
N_TILE = 512
HALVES = H_SIZE // N_TILE
BIAS_WORDS = H_SIZE // 2 // P
WARM_UPS = 4
TO_VAR = 1.0 / (N_TILE * N_TILE * H_SIZE)
HALF_DISTANCE = 16.0
QUADRANTS = 4

FLOPS = 2 * P * (I_SIZE + H_SIZE) * H_SIZE


def tile_layernormgrucell_pb_s_kernel(
    tc, x, h, r, z, W_in_words, W_in_scales, b_in, W_hn_words, W_hn_scales, b_hn, out
):
    nc = tc.nc
    with ExitStack() as ctx:
        keep = ctx.enter_context(tc.tile_pool(name="keep", bufs=1))
        psum = ctx.enter_context(tc.psum_pool(name="psum", bufs=7))
        ctx.enter_context(tc.manual_schedule())

        idle = keep.tile([P, P], F32)
        nc.gpsimd.memset(idle[:], 0.0)
        x_sb = keep.tile([P, I_SIZE], BF16)
        h_sb = keep.tile([P, H_SIZE], BF16)
        b_in_words = keep.tile([P, BIAS_WORDS * 2], BF16)
        b_hn_words = keep.tile([P, BIAS_WORDS * 2], BF16)
        w_scales = keep.tile([P, PASSES, H_SIZE], U8, align_bytes=64)
        nc.vector.memset(w_scales[:, 0, :].bitcast(I32), 0)
        nc.gpsimd.dma_start(out=b_hn_words[:], in_=b_hn.rearrange("(w e) -> w e", w=P))

        w_words = keep.tile([P, PASSES, 2 * H_SIZE], U8, align_bytes=64)
        nc.scalar.dma_start(out=b_in_words[:], in_=b_in.rearrange("(w e) -> w e", w=P))
        for q in range(QUADRANTS):
            nc.sync.dma_start(
                out=w_scales[32 * q : 32 * q + 4, 0, :].bitcast(I32),
                in_=W_in_scales[0, 4 * q : 4 * q + 4, :].bitcast(I32),
            )
        nc.scalar.dma_start(out=x_sb[:], in_=x)
        nc.scalar.dma_start(out=h_sb[:], in_=h)
        nc.sync.dma_start(out=w_words[:, 0, :].bitcast(I32), in_=W_in_words[0].bitcast(I32))
        nc.vector.memset(w_scales[:, 1:PASSES, :].bitcast(I32), 0)
        nc.sync.dma_start(
            out=w_words[:, 1:PASSES, :].bitcast(I32),
            in_=W_hn_words.bitcast(I32).rearrange("g p n -> p g n"),
        )
        for q in range(QUADRANTS):
            nc.sync.dma_start(
                out=w_scales[32 * q : 32 * q + 4, 1:PASSES, :].bitcast(I32),
                in_=W_hn_scales[:, 4 * q : 4 * q + 4, :].bitcast(I32).rearrange("g s n -> s g n"),
            )

        warm = keep.tile([P, 1], F32)
        nc.vector.memset(warm[:], 1.0)
        nc.scalar.activation(out=warm[:], in_=warm[:], func=ACT.Abs_reciprocal_sqrt)

        ident = keep.tile([P, P], F32)
        make_identity(nc, ident[:])
        z_sb = keep.tile([P, H_SIZE], BF16)
        r_sb = keep.tile([P, H_SIZE], BF16)
        nc.gpsimd.dma_start(out=z_sb[:], in_=z)
        nc.gpsimd.dma_start(out=r_sb[:], in_=r)

        grouped = keep.tile([P, PASSES, P * PACK], BF16, align_bytes=64)
        a_codes = keep.tile([P, PASSES, P], U32, align_bytes=64)
        a_scales = keep.tile([P, PASSES, P], U8, align_bytes=64)
        pass_words = [
            x_sb[:].bitcast(F32),
            h_sb[:].bitcast(F32)[:, 0:WORDS],
            h_sb[:].bitcast(F32)[:, WORDS : 2 * WORDS],
        ]

        bias = keep.tile([P, 2, H_SIZE], BF16)

        def spread_bias(bias_words):
            spread = psum.tile([P, BIAS_WORDS, P], F32, tag="bank")
            for m in range(BIAS_WORDS):
                nc.tensor.transpose(
                    spread[:, m, :], bias_words[:].bitcast(F32)[:, m : m + 1].to_broadcast([P, P]), ident[:]
                )
            return spread

        def collect_bias(side, spread):
            nc.scalar.copy(
                out=bias[:, side, :].bitcast(F32).rearrange("p (w m) -> p w m", m=BIAS_WORDS),
                in_=spread[:].rearrange("p m w -> p w m"),
            )

        def quantise(c):
            nc.vector.quantize_mx(
                out=a_codes[:, c, :].bitcast(FP8X4), scales=a_scales[:, c, :], in_=grouped[:, c, :]
            )

        unread = psum.tile([P, 4, P], F32, tag="unread", bufs=1)

        def keep_warm(i):
            nc.tensor.matmul(unread[:, i % 4, :], lhsT=idle[:], rhs=idle[:], start=True, stop=True)

        for i in range(WARM_UPS):
            keep_warm(i)

        for c in range(PASSES):
            flipped = psum.tile([P, 2, P], F32, tag="bank")
            for u in range(2):
                nc.tensor.transpose(flipped[:, u, :], pass_words[c][:, u:WORDS:2], ident[:])
            side_by_side = grouped[:, c, :].bitcast(F32).rearrange("p (b u) -> p b u", u=2)
            if c == 2:
                nc.vector.tensor_copy(out=side_by_side, in_=flipped[:].rearrange("p u b -> p b u"))
            else:
                nc.scalar.copy(out=side_by_side, in_=flipped[:].rearrange("p u b -> p b u"))
            if c == 0:
                quantise(0)
                spread_in = spread_bias(b_in_words)
        keep_warm(0)
        collect_bias(0, spread_in)
        quantise(1)
        quantise(2)

        passes_of_side = [[0], [1, 2]]
        pre = keep.tile([P, 2, H_SIZE], F32)
        sums = keep.tile([P, 2, 4], F32)
        squares = keep.tile([P, 2, H_SIZE], F32)
        sq_sums = keep.tile([P, 2, 4], F32)

        def product(side, cols):
            width = cols.stop - cols.start
            acc = psum.tile([P, width], F32, tag="bank")
            for c in passes_of_side[side]:
                nc.tensor.matmul_mx(
                    out=acc[:],
                    lhsT=a_codes[:, c, :].bitcast(FP8X4),
                    lhsT_scale=a_scales[:, c, :],
                    rhs=w_words[:, c, 2 * cols.start : 2 * cols.stop].bitcast(FP4X4),
                    rhs_scale=w_scales[:, c, cols],
                    start=(c == passes_of_side[side][0]),
                    stop=(c == passes_of_side[side][-1]),
                )
            return acc

        def add_bias(side, i, acc):
            cols = pieces[side][i]
            nc.vector.scalar_tensor_tensor(
                out=pre[:, side, cols],
                in0=acc[:],
                scalar=1.0,
                in1=bias[:, side, cols],
                op0=ALU.mult,
                op1=ALU.add,
                accum_out=sums[:, side, i : i + 1],
            )

        half = [slice(0, N_TILE), slice(N_TILE, H_SIZE)]
        quarters = [slice(c, c + 256) for c in range(0, H_SIZE, 256)]
        pieces = [half, half]

        acc_in = [product(0, cols) for cols in half]
        collect_bias(1, spread_bias(b_hn_words))
        acc_hn = [product(1, cols) for cols in half]

        def square_deviations(side, j):
            nc.scalar.activation(
                out=squares[:, side, half[j]], in_=pre[:, side, half[j]], func=ACT.Square,
                bias=sums[:, side, j : j + 1], scale=-float(N_TILE), accum_out=sq_sums[:, side, j : j + 1],
            )

        def negative_mean(engine, out, side):
            engine.tensor_scalar(
                out=out, in0=sums[:, side, 0:1], scalar1=sums[:, side, 1:2], scalar2=-1.0 / H_SIZE,
                op0=ALU.add, op1=ALU.mult,
            )

        scale_in = keep.tile([P, 1], F32)
        ratio = keep.tile([P, 1], F32)
        for j in range(HALVES):
            add_bias(0, j, acc_in[j])
            square_deviations(0, j)

        def distance(engine, dist, side):
            engine.tensor_scalar(
                out=dist, in0=sums[:, side, 0:1], scalar1=sums[:, side, 1:2], scalar2=HALF_DISTANCE,
                op0=ALU.subtract, op1=ALU.mult,
            )

        def distance_squared(engine, rest, dist):
            engine.tensor_scalar(
                out=rest, in0=dist, scalar1=dist, scalar2=EPS / TO_VAR, op0=ALU.mult, op1=ALU.add
            )

        z_times_h = keep.tile([P, H_SIZE], F32)

        def state_term(engine, cols):
            engine.tensor_tensor(out=z_times_h[:, cols], in0=z_sb[:, cols], in1=h_sb[:, cols], op=ALU.mult)

        state_term(nc.gpsimd, quarters[0])
        side_0 = keep.tile([P, 4], F32)
        dist_in, rest_in, bias_in, mean_in = [side_0[:, i : i + 1] for i in range(4)]
        distance(nc.gpsimd, dist_in, 0)
        distance_squared(nc.gpsimd, rest_in, dist_in)
        nc.gpsimd.tensor_scalar(
            out=bias_in, in0=sq_sums[:, 0, 0:1], scalar1=rest_in, scalar2=TO_VAR, op0=ALU.add, op1=ALU.mult
        )
        negative_mean(nc.gpsimd, mean_in, 0)
        state_term(nc.gpsimd, quarters[1])
        state_term(nc.gpsimd, quarters[2])

        add_bias(1, 0, acc_hn[0])
        square_deviations(1, 0)
        nc.scalar.activation(
            out=scale_in[:], in_=sq_sums[:, 0, 1:2], func=ACT.Abs_reciprocal_sqrt, scale=TO_VAR, bias=bias_in
        )
        add_bias(1, 1, acc_hn[1])
        square_deviations(1, 1)

        side_1 = keep.tile([P, 5], F32)
        dist_hn, rest_hn, mean_hn, to_ratio, bias_hn = [side_1[:, i : i + 1] for i in range(5)]
        gated = keep.tile([P, H_SIZE], F32)

        distance(nc.vector, dist_hn, 1)
        negative_mean(nc.vector, mean_hn, 1)
        nc.vector.tensor_scalar(
            out=to_ratio, in0=scale_in[:], scalar1=scale_in[:], scalar2=TO_VAR, op0=ALU.mult, op1=ALU.mult
        )
        distance_squared(nc.vector, rest_hn, dist_hn)
        nc.vector.tensor_scalar(
            out=bias_hn, in0=sq_sums[:, 1, 0:1], scalar1=rest_hn, scalar2=to_ratio, op0=ALU.add, op1=ALU.mult
        )
        for cols in half:
            nc.vector.scalar_tensor_tensor(
                out=gated[:, cols], in0=pre[:, 1, cols], scalar=mean_hn, in1=r_sb[:, cols],
                op0=ALU.add, op1=ALU.mult,
            )
        nc.scalar.activation(
            out=ratio[:], in_=sq_sums[:, 1, 1:2], func=ACT.Abs_reciprocal_sqrt, scale=to_ratio, bias=bias_hn
        )
        nc.scalar.activation(out=warm[:], in_=warm[:], func=ACT.Tanh)

        shift = keep.tile([P, 1], F32)
        arg = keep.tile([P, H_SIZE], F32)
        cand = keep.tile([P, H_SIZE], F32)
        part = keep.tile([P, H_SIZE], F32)
        res = keep.tile([P, H_SIZE], F32)
        nc.vector.tensor_scalar(
            out=shift[:], in0=mean_in, scalar1=scale_in[:], scalar2=None, op0=ALU.mult
        )
        for cols in half:
            nc.vector.scalar_tensor_tensor(
                out=arg[:, cols], in0=gated[:, cols], scalar=ratio[:], in1=pre[:, 0, cols],
                op0=ALU.mult, op1=ALU.add,
            )

        state_term(nc.vector, quarters[3])
        for cols in quarters:
            nc.scalar.activation(
                out=cand[:, cols], in_=arg[:, cols], func=ACT.Tanh, bias=shift[:], scale=scale_in[:]
            )

        def blend(cols):
            nc.vector.scalar_tensor_tensor(
                out=part[:, cols], in0=z_sb[:, cols], scalar=-1.0, in1=cand[:, cols],
                op0=ALU.add, op1=ALU.mult,
            )

        def finish(cols):
            nc.vector.tensor_tensor(out=res[:, cols], in0=z_times_h[:, cols], in1=part[:, cols], op=ALU.subtract)

        def store(cols):
            nc.sync.dma_start(out=out[:, cols], in_=res[:, cols])

        blend(quarters[0])
        blend(quarters[1])
        finish(quarters[0])
        blend(quarters[2])
        finish(quarters[1])
        store(half[0])
        blend(quarters[3])
        finish(quarters[2])
        store(quarters[2])
        finish(quarters[3])
        store(quarters[3])
